import numpy as np
import ml_dtypes


def mxq(x, axis, fmt="e4m3"):
    dtype, down = {"e4m3": (ml_dtypes.float8_e4m3fn, 7), "e5m2": (ml_dtypes.float8_e5m2, 14)}[fmt]
    v = np.moveaxis(np.asarray(x, np.float32).astype(ml_dtypes.bfloat16).astype(np.float64), axis, -1)
    blocks = v.reshape(v.shape[:-1] + (-1, 32))
    amax = np.abs(blocks).max(-1, keepdims=True)
    byte = np.maximum(np.where(amax > 0, np.frexp(amax)[1] - 1 + 127, 0) - down, 1)
    scale = np.exp2(byte - 127.0)
    codes = (blocks / scale).astype(np.float32).astype(dtype).astype(np.float64)
    return np.moveaxis((codes * scale).reshape(v.shape), -1, axis)


WIDE = False


def mx_kscale(k):
    if not WIDE:
        return np.ones(k)
    levels = np.array([10, -10, 5, -5, 0])
    a = np.random.permutation(np.resize(levels, k // 512 * 4)).reshape(k // 512, 4)
    idx = np.arange(k)
    return np.exp2(a[idx // 512, idx % 128 // 32])


BF16 = ml_dtypes.bfloat16


def bf(x):
    return np.asarray(x, np.float32).astype(BF16)


def f64(x):
    return np.asarray(x).astype(np.float64)


B, C, D, T, H, W, P = 1, 1024, 512, 8, 16, 16, 2
N = T * H * W
BN_EPS = 1e-5


def setup_inputs():
    s = mx_kscale(D)
    return {"y": bf(np.random.standard_normal((B, D, T, H, W)) * 0.3 * np.sqrt(D) * s[None, :, None, None, None]),
            "w_w": bf(np.random.standard_normal((C, D)) / (0.3 * D) / s[None, :]),
            "w_b": bf(np.random.standard_normal(C) * 0.3),
            "bn_gamma": bf(np.random.standard_normal(C))}


def reference(y, w_w, w_b, bn_gamma):
    wy = (mxq(f64(w_w), 1, "e4m3") @ mxq(f64(y).reshape(B, D, N), 1, "e4m3")) + f64(w_b)[None, :, None]
    wy = wy.reshape(B, C, T, H, W)
    mean = wy.mean(axis=(0, 2, 3, 4))
    var = wy.var(axis=(0, 2, 3, 4))
    return wy, mean, f64(bn_gamma) / np.sqrt(var + BN_EPS)

@@ -1,0 +1,236 @@
+from contextlib import ExitStack
+
+import concourse.mybir as mybir
+from concourse.masks import make_identity
+
+FP8X4 = mybir.dt.float8_e4m3fn_x4
+BF16 = mybir.dt.bfloat16
+F32 = mybir.dt.float32
+U32 = mybir.dt.uint32
+U8 = mybir.dt.uint8
+ACT = mybir.ActivationFunctionType
+ALU = mybir.AluOpType
+
+P = 128
+PACK = 4
+D_IN = P * PACK
+CHANNELS = 1024
+POSITIONS = 2048
+CH_TILES = CHANNELS // P
+CHUNK = 512
+CHUNKS = POSITIONS // CHUNK
+PAIR = 2
+PAIRS = CH_TILES // PAIR
+RUN = 4
+VECTOR_COLS = 384
+GPSIMD_PIECE = 128
+BN_STATS_DIM = 6
+TRIPLE = 3
+QUANTISE_NEXT_AFTER_TILE = 2
+BN_EPS = 1e-5
+
+FLOPS = 2 * CHANNELS * D_IN * POSITIONS
+
+
+def tile_nonlocalblocknd_pc_kernel(tc, y, w_w, w_b, bn_gamma, out_0, out_1, out_2):
+    nc = tc.nc
+
+    y_rows = y[0].rearrange("(p j) t h w -> p j (t h w)", j=PACK)
+    w_rows = w_w.rearrange("(p m) d -> p (m d)", m=CH_TILES)
+    wy_rows = out_0[0].rearrange("(p m) t h w -> p m (t h w)", m=CH_TILES)
+
+    with ExitStack() as ctx:
+        consts = ctx.enter_context(tc.tile_pool(name="consts", bufs=1))
+        y_pool = ctx.enter_context(tc.tile_pool(name="y_pool", bufs=CHUNKS))
+        w_pool = ctx.enter_context(tc.tile_pool(name="w_pool", bufs=PAIRS))
+        handoff = ctx.enter_context(tc.tile_pool(name="handoff", bufs=1))
+        wy_pool = ctx.enter_context(tc.tile_pool(name="wy_pool", bufs=PAIRS * CHUNKS))
+        psum_w = ctx.enter_context(tc.psum_pool(name="psum_w", bufs=2))
+        psum_acc = ctx.enter_context(tc.psum_pool(name="psum_acc", bufs=6))
+        ctx.enter_context(tc.manual_schedule())
+
+        bias_bf16 = consts.tile([P, CH_TILES], BF16)
+        nc.scalar.dma_start(out=bias_bf16[:], in_=w_b.rearrange("(p m) -> p m", m=CH_TILES))
+        gamma_bf16 = consts.tile([P, CH_TILES], BF16)
+        nc.scalar.dma_start(out=gamma_bf16[:], in_=bn_gamma.rearrange("(p m) -> p m", m=CH_TILES))
+
+        def load_y_chunk(c):
+            y_raw = y_pool.tile([P, PACK, CHUNK], BF16)
+            nc.sync.dma_start(out=y_raw[:], in_=y_rows[:, :, c * CHUNK : (c + 1) * CHUNK])
+            return y_raw
+
+        def load_w_pair(pair):
+            width = PAIR * D_IN
+            w_raw = w_pool.tile([P, width], BF16)
+            nc.sync.dma_start(out=w_raw[:], in_=w_rows[:, pair * width : (pair + 1) * width])
+            return w_raw
+
+        y_raws = {}
+        w_raws = {}
+        w_raws[0] = load_w_pair(0)
+        w_raws[1] = load_w_pair(1)
+        y_raws[0] = load_y_chunk(0)
+        w_raws[2] = load_w_pair(2)
+        w_raws[3] = load_w_pair(3)
+        y_raws[1] = load_y_chunk(1)
+        y_raws[2] = load_y_chunk(2)
+        y_raws[3] = load_y_chunk(3)
+
+        eps = consts.tile([P, 1], F32)
+        nc.vector.memset(eps[:], BN_EPS)
+        stats = consts.tile([P, CH_TILES, CHUNKS, BN_STATS_DIM], F32)
+        nc.vector.memset(stats[:], float(CHUNK))
+        table_warmer = consts.tile([P, 1], F32)
+        nc.scalar.activation(out=table_warmer[:], in_=eps[:], func=ACT.Abs_reciprocal_sqrt)
+        identity = consts.tile([P, P], F32)
+        make_identity(nc, identity[:])
+
+        def regroup_y_chunk(c):
+            y_grouped = y_pool.tile([P, CHUNK, PACK], BF16, align_bytes=64)
+            src = y_raws[c][:].rearrange("p j (c i) -> p c j i", i=RUN)
+            dst = y_grouped[:].rearrange("p (c i) j -> p c j i", i=RUN)
+            split = VECTOR_COLS // RUN
+            nc.vector.tensor_copy(out=dst[:, :split], in_=src[:, :split])
+            nc.scalar.copy(out=dst[:, split:], in_=src[:, split:])
+            return y_grouped
+
+        def regroup_y_chunk_on_gpsimd(c):
+            y_grouped = handoff.tile([P, CHUNK, PACK], BF16, align_bytes=64)
+            gpsimd_cols = CHUNK
+            if c == 1:
+                gpsimd_cols = CHUNK - GPSIMD_PIECE
+                src = y_raws[c][:].rearrange("p j (c i) -> p c j i", i=RUN)
+                dst = y_grouped[:].rearrange("p (c i) j -> p c j i", i=RUN)
+                nc.vector.tensor_copy(out=dst[:, gpsimd_cols // RUN :], in_=src[:, gpsimd_cols // RUN :])
+            for first in range(0, gpsimd_cols, GPSIMD_PIECE):
+                cols = slice(first, first + GPSIMD_PIECE)
+                nc.gpsimd.tensor_scalar(
+                    out=y_grouped[:, cols, :],
+                    in0=y_raws[c][:, :, cols].rearrange("p j n -> p n j"),
+                    scalar1=1.0,
+                    scalar2=0.0,
+                    op0=ALU.mult,
+                    op1=ALU.add,
+                )
+            return y_grouped
+
+        def quantise_y_chunk(y_grouped):
+            y_codes = y_pool.tile([P, CHUNK], U32, align_bytes=64)
+            y_scales = y_pool.tile([P, CHUNK], U8, align_bytes=64)
+            nc.vector.quantize_mx(
+                out=y_codes[:].bitcast(FP8X4),
+                scales=y_scales[:],
+                in_=y_grouped[:].rearrange("p n j -> p (n j)"),
+            )
+            return y_codes, y_scales
+
+        def transpose_w_pair(pair):
+            words = w_raws[pair][:].bitcast(F32).rearrange("c (t p u) -> c t u p", p=P, u=2)
+            w_t = psum_w.tile([P, PAIR, 2, P], F32)
+            for t in range(PAIR):
+                for u in range(2):
+                    nc.tensor.transpose(w_t[:, t, u, :], words[:, t, u, :], identity[:])
+            w_grouped = w_pool.tile([P, PAIR * P * PACK], BF16, align_bytes=64)
+            nc.scalar.copy(
+                out=w_grouped[:].bitcast(F32).rearrange("p (t c u) -> p t c u", t=PAIR, u=2),
+                in_=w_t[:].rearrange("p t u c -> p t c u"),
+            )
+            return w_grouped
+
+        def quantise_w_pair(w_grouped):
+            w_codes = w_pool.tile([P, PAIR * P], U32, align_bytes=64)
+            w_scales = w_pool.tile([P, PAIR * P], U8, align_bytes=64)
+            nc.vector.quantize_mx(out=w_codes[:].bitcast(FP8X4), scales=w_scales[:], in_=w_grouped[:])
+            return w_codes, w_scales
+
+
+        mean_var = consts.tile([P, 2, CH_TILES], F32)
+        last_sum = consts.tile([P, 1], F32)
+        squares = consts.tile([P, CHUNK], BF16)
+        y_mx = {}
+        w_mx = {}
+        last_tile = (CH_TILES - 1, CHUNKS - 1)
+
+        def aggregate_pair(pair):
+            for m in range(pair * PAIR, (pair + 1) * PAIR):
+                used = CHUNKS * BN_STATS_DIM - (TRIPLE if m == last_tile[0] else 0)
+                nc.vector.bn_aggr(out=mean_var[:, :, m], in_=stats[:, m].rearrange("p c s -> p (c s)")[:, :used])
+
+        def scalar_stats(wy_last):
+            m, c = last_tile
+            tile_mean = stats[:, m, c, 1:2]
+            nc.scalar.activation(out=tile_mean, in_=last_sum[:], func=ACT.Copy, scale=1.0 / CHUNK)
+            nc.scalar.activation(
+                out=squares[:], in_=wy_last, func=ACT.Square, bias=tile_mean, scale=-1.0, accum_out=stats[:, m, c, 2:3]
+            )
+
+        def multiply(m, c, wy):
+            pair, t = divmod(m, PAIR)
+            w_codes, w_scales = w_mx[pair]
+            y_codes, y_scales = y_mx[c]
+            w_cols = slice(t * P, (t + 1) * P)
+            acc = psum_acc.tile([P, CHUNK], F32)
+            nc.tensor.matmul_mx(
+                out=acc[:],
+                lhsT=w_codes[:, w_cols].bitcast(FP8X4),
+                lhsT_scale=w_scales[:, w_cols],
+                rhs=y_codes[:].bitcast(FP8X4),
+                rhs_scale=y_scales[:],
+                start=True,
+                stop=True,
+            )
+            if (m, c) == last_tile:
+                nc.scalar.activation(
+                    out=wy[:, t, :],
+                    in_=acc[:],
+                    func=ACT.Identity,
+                    bias=bias_bf16[:, m : m + 1],
+                    scale=1.0,
+                    accum_out=last_sum[:],
+                )
+            else:
+                nc.scalar.activation(
+                    out=wy[:, t, :], in_=acc[:], func=ACT.Identity, bias=bias_bf16[:, m : m + 1], scale=1.0
+                )
+                nc.vector.bn_stats(out=stats[:, m, c, :], in_=wy[:, t, :])
+
+        w_grouped_0 = transpose_w_pair(0)
+        w_grouped_1 = transpose_w_pair(1)
+        w_mx[0] = quantise_w_pair(w_grouped_0)
+        y_grouped_0 = regroup_y_chunk(0)
+        y_mx[0] = quantise_y_chunk(y_grouped_0)
+        w_mx[1] = quantise_w_pair(w_grouped_1)
+        w_grouped_2 = transpose_w_pair(2)
+        w_mx[2] = quantise_w_pair(w_grouped_2)
+        w_grouped_3 = transpose_w_pair(3)
+        w_mx[3] = quantise_w_pair(w_grouped_3)
+        y_grouped_next = regroup_y_chunk_on_gpsimd(1)
+
+        for c in range(CHUNKS):
+            positions = slice(c * CHUNK, (c + 1) * CHUNK)
+            for m in range(CH_TILES):
+                pair, t = divmod(m, PAIR)
+                if t == 0:
+                    wy = wy_pool.tile([P, PAIR, CHUNK], F32)
+                multiply(m, c, wy)
+                if (pair, c) == (PAIRS - 1, CHUNKS - 1):
+                    nc.sync.dma_start(out=wy_rows[:, m, positions], in_=wy[:, t, :])
+                elif t == PAIR - 1:
+                    nc.sync.dma_start(out=wy_rows[:, m - t : m + 1, positions], in_=wy[:])
+                if m == QUANTISE_NEXT_AFTER_TILE and c + 1 < CHUNKS:
+                    y_mx[c + 1] = quantise_y_chunk(y_grouped_next)
+                    if c + 2 < CHUNKS:
+                        y_grouped_next = regroup_y_chunk_on_gpsimd(c + 2)
+                if c == CHUNKS - 1 and t == PAIR - 1 and pair >= 1:
+                    aggregate_pair(pair - 1)
+        scalar_stats(wy[:, PAIR - 1, :])
+        aggregate_pair(PAIRS - 1)
+
+        nc.sync.dma_start(out=out_1.rearrange("(p m) -> p m", m=CH_TILES), in_=mean_var[:, 0, :])
+        inv_std = consts.tile([P, CH_TILES], F32)
+        nc.scalar.activation(
+            out=inv_std[:], in_=mean_var[:, 1, :], func=ACT.Abs_reciprocal_sqrt, bias=eps[:], scale=1.0
+        )
+        gain = consts.tile([P, CH_TILES], F32)
+        nc.vector.tensor_mul(out=gain[:], in0=inv_std[:], in1=gamma_bf16[:])
+        nc.sync.dma_start(out=out_2.rearrange("(p m) -> p m", m=CH_TILES), in_=gain[:])

@@ -26,7 +26,7 @@ VECTOR_COLS = 384
 GPSIMD_PIECE = 128
 BN_STATS_DIM = 6
 TRIPLE = 3
-QUANTISE_NEXT_AFTER_TILE = 2
+PREPARE_NEXT_AFTER_TILE = 3
 BN_EPS = 1e-5
 
 FLOPS = 2 * CHANNELS * D_IN * POSITIONS
@@ -68,11 +68,11 @@ def tile_nonlocalblocknd_pc_kernel(tc, y, w_w, w_b, bn_gamma, out_0, out_1, out_
         y_raws = {}
         w_raws = {}
         w_raws[0] = load_w_pair(0)
-        w_raws[1] = load_w_pair(1)
         y_raws[0] = load_y_chunk(0)
+        w_raws[1] = load_w_pair(1)
         w_raws[2] = load_w_pair(2)
-        w_raws[3] = load_w_pair(3)
         y_raws[1] = load_y_chunk(1)
+        w_raws[3] = load_w_pair(3)
         y_raws[2] = load_y_chunk(2)
         y_raws[3] = load_y_chunk(3)
 
@@ -96,13 +96,7 @@ def tile_nonlocalblocknd_pc_kernel(tc, y, w_w, w_b, bn_gamma, out_0, out_1, out_
 
         def regroup_y_chunk_on_gpsimd(c):
             y_grouped = handoff.tile([P, CHUNK, PACK], BF16, align_bytes=64)
-            gpsimd_cols = CHUNK
-            if c == 1:
-                gpsimd_cols = CHUNK - GPSIMD_PIECE
-                src = y_raws[c][:].rearrange("p j (c i) -> p c j i", i=RUN)
-                dst = y_grouped[:].rearrange("p (c i) j -> p c j i", i=RUN)
-                nc.vector.tensor_copy(out=dst[:, gpsimd_cols // RUN :], in_=src[:, gpsimd_cols // RUN :])
-            for first in range(0, gpsimd_cols, GPSIMD_PIECE):
+            for first in range(0, CHUNK, GPSIMD_PIECE):
                 cols = slice(first, first + GPSIMD_PIECE)
                 nc.gpsimd.tensor_scalar(
                     out=y_grouped[:, cols, :],
@@ -195,15 +189,13 @@ def tile_nonlocalblocknd_pc_kernel(tc, y, w_w, w_b, bn_gamma, out_0, out_1, out_
                 nc.vector.bn_stats(out=stats[:, m, c, :], in_=wy[:, t, :])
 
         w_grouped_0 = transpose_w_pair(0)
-        w_grouped_1 = transpose_w_pair(1)
-        w_mx[0] = quantise_w_pair(w_grouped_0)
         y_grouped_0 = regroup_y_chunk(0)
+        w_mx[0] = quantise_w_pair(w_grouped_0)
+        w_grouped_1 = transpose_w_pair(1)
         y_mx[0] = quantise_y_chunk(y_grouped_0)
-        w_mx[1] = quantise_w_pair(w_grouped_1)
         w_grouped_2 = transpose_w_pair(2)
+        w_mx[1] = quantise_w_pair(w_grouped_1)
         w_mx[2] = quantise_w_pair(w_grouped_2)
-        w_grouped_3 = transpose_w_pair(3)
-        w_mx[3] = quantise_w_pair(w_grouped_3)
         y_grouped_next = regroup_y_chunk_on_gpsimd(1)
 
         for c in range(CHUNKS):
@@ -217,7 +209,9 @@ def tile_nonlocalblocknd_pc_kernel(tc, y, w_w, w_b, bn_gamma, out_0, out_1, out_
                     nc.sync.dma_start(out=wy_rows[:, m, positions], in_=wy[:, t, :])
                 elif t == PAIR - 1:
                     nc.sync.dma_start(out=wy_rows[:, m - t : m + 1, positions], in_=wy[:])
-                if m == QUANTISE_NEXT_AFTER_TILE and c + 1 < CHUNKS:
+                if m == PREPARE_NEXT_AFTER_TILE and c == 0:
+                    w_mx[PAIRS - 1] = quantise_w_pair(transpose_w_pair(PAIRS - 1))
+                if m == PREPARE_NEXT_AFTER_TILE and c + 1 < CHUNKS:
                     y_mx[c + 1] = quantise_y_chunk(y_grouped_next)
                     if c + 2 < CHUNKS:
                         y_grouped_next = regroup_y_chunk_on_gpsimd(c + 2)

@@ -76,6 +76,8 @@ def tile_nonlocalblocknd_pc_kernel(tc, y, w_w, w_b, bn_gamma, out_0, out_1, out_
         y_raws[2] = load_y_chunk(2)
         y_raws[3] = load_y_chunk(3)
 
+        zeros = consts.tile([P, CHUNK], BF16)
+        nc.gpsimd.memset(zeros[:], 0.0)
         eps = consts.tile([P, 1], F32)
         nc.vector.memset(eps[:], BN_EPS)
         stats = consts.tile([P, CH_TILES, CHUNKS, BN_STATS_DIM], F32)
@@ -188,12 +190,20 @@ def tile_nonlocalblocknd_pc_kernel(tc, y, w_w, w_b, bn_gamma, out_0, out_1, out_
                 )
                 nc.vector.bn_stats(out=stats[:, m, c, :], in_=wy[:, t, :])
 
+        def keep_tensor_engine_busy(matmuls):
+            acc = psum_acc.tile([P, CHUNK], F32)
+            for i in range(matmuls):
+                nc.tensor.matmul(acc[:], lhsT=zeros[:, :P], rhs=zeros[:], start=True, stop=True)
+
+        keep_tensor_engine_busy(4)
         w_grouped_0 = transpose_w_pair(0)
+        keep_tensor_engine_busy(3)
         y_grouped_0 = regroup_y_chunk(0)
         w_mx[0] = quantise_w_pair(w_grouped_0)
         w_grouped_1 = transpose_w_pair(1)
         y_mx[0] = quantise_y_chunk(y_grouped_0)
         w_grouped_2 = transpose_w_pair(2)
+        keep_tensor_engine_busy(1)
         w_mx[1] = quantise_w_pair(w_grouped_1)
         w_mx[2] = quantise_w_pair(w_grouped_2)
         y_grouped_next = regroup_y_chunk_on_gpsimd(1)

@@ -230,11 +230,11 @@ def tile_nonlocalblocknd_pc_kernel(tc, y, w_w, w_b, bn_gamma, out_0, out_1, out_
         scalar_stats(wy[:, PAIR - 1, :])
         aggregate_pair(PAIRS - 1)
 
-        nc.sync.dma_start(out=out_1.rearrange("(p m) -> p m", m=CH_TILES), in_=mean_var[:, 0, :])
         inv_std = consts.tile([P, CH_TILES], F32)
         nc.scalar.activation(
             out=inv_std[:], in_=mean_var[:, 1, :], func=ACT.Abs_reciprocal_sqrt, bias=eps[:], scale=1.0
         )
+        nc.scalar.dma_start(out=out_1.rearrange("(p m) -> p m", m=CH_TILES), in_=mean_var[:, 0, :])
         gain = consts.tile([P, CH_TILES], F32)
         nc.vector.tensor_mul(out=gain[:], in0=inv_std[:], in1=gamma_bf16[:])
-        nc.sync.dma_start(out=out_2.rearrange("(p m) -> p m", m=CH_TILES), in_=gain[:])
+        nc.scalar.dma_start(out=out_2.rearrange("(p m) -> p m", m=CH_TILES), in_=gain[:])

@@ -26,6 +26,8 @@ VECTOR_COLS = 384
 GPSIMD_PIECE = 128
 BN_STATS_DIM = 6
 TRIPLE = 3
+STATS_FIRST = 6
+STATS_ROW = 32
 PREPARE_NEXT_AFTER_TILE = 3
 BN_EPS = 1e-5
 
@@ -49,11 +51,6 @@ def tile_nonlocalblocknd_pc_kernel(tc, y, w_w, w_b, bn_gamma, out_0, out_1, out_
         psum_acc = ctx.enter_context(tc.psum_pool(name="psum_acc", bufs=6))
         ctx.enter_context(tc.manual_schedule())
 
-        bias_bf16 = consts.tile([P, CH_TILES], BF16)
-        nc.scalar.dma_start(out=bias_bf16[:], in_=w_b.rearrange("(p m) -> p m", m=CH_TILES))
-        gamma_bf16 = consts.tile([P, CH_TILES], BF16)
-        nc.scalar.dma_start(out=gamma_bf16[:], in_=bn_gamma.rearrange("(p m) -> p m", m=CH_TILES))
-
         def load_y_chunk(c):
             y_raw = y_pool.tile([P, PACK, CHUNK], BF16)
             nc.sync.dma_start(out=y_raw[:], in_=y_rows[:, :, c * CHUNK : (c + 1) * CHUNK])
@@ -73,17 +70,21 @@ def tile_nonlocalblocknd_pc_kernel(tc, y, w_w, w_b, bn_gamma, out_0, out_1, out_
         w_raws[2] = load_w_pair(2)
         y_raws[1] = load_y_chunk(1)
         w_raws[3] = load_w_pair(3)
-        y_raws[2] = load_y_chunk(2)
-        y_raws[3] = load_y_chunk(3)
+        y_late = consts.tile([P, PACK, 2 * CHUNK], BF16)
+        nc.sync.dma_start(out=y_late[:], in_=y_rows[:, :, 2 * CHUNK :])
 
         zeros = consts.tile([P, CHUNK], BF16)
         nc.gpsimd.memset(zeros[:], 0.0)
         eps = consts.tile([P, 1], F32)
         nc.vector.memset(eps[:], BN_EPS)
-        stats = consts.tile([P, CH_TILES, CHUNKS, BN_STATS_DIM], F32)
+        stats = consts.tile([P, CH_TILES, STATS_ROW], F32)
         nc.vector.memset(stats[:], float(CHUNK))
         table_warmer = consts.tile([P, 1], F32)
         nc.scalar.activation(out=table_warmer[:], in_=eps[:], func=ACT.Abs_reciprocal_sqrt)
+        bias_bf16 = consts.tile([P, CH_TILES], BF16)
+        nc.scalar.dma_start(out=bias_bf16[:], in_=w_b.rearrange("(p m) -> p m", m=CH_TILES))
+        gamma_bf16 = consts.tile([P, CH_TILES], BF16)
+        nc.scalar.dma_start(out=gamma_bf16[:], in_=bn_gamma.rearrange("(p m) -> p m", m=CH_TILES))
         identity = consts.tile([P, P], F32)
         make_identity(nc, identity[:])
 
@@ -98,11 +99,12 @@ def tile_nonlocalblocknd_pc_kernel(tc, y, w_w, w_b, bn_gamma, out_0, out_1, out_
 
         def regroup_y_chunk_on_gpsimd(c):
             y_grouped = handoff.tile([P, CHUNK, PACK], BF16, align_bytes=64)
+            rows = y_raws[c][:] if c < 2 else y_late[:, :, (c - 2) * CHUNK : (c - 1) * CHUNK]
             for first in range(0, CHUNK, GPSIMD_PIECE):
                 cols = slice(first, first + GPSIMD_PIECE)
                 nc.gpsimd.tensor_scalar(
                     out=y_grouped[:, cols, :],
-                    in0=y_raws[c][:, :, cols].rearrange("p j n -> p n j"),
+                    in0=rows[:, :, cols].rearrange("p j n -> p n j"),
                     scalar1=1.0,
                     scalar2=0.0,
                     op0=ALU.mult,
@@ -141,23 +143,35 @@ def tile_nonlocalblocknd_pc_kernel(tc, y, w_w, w_b, bn_gamma, out_0, out_1, out_
 
 
         mean_var = consts.tile([P, 2, CH_TILES], F32)
-        last_sum = consts.tile([P, 1], F32)
+        last_sums = consts.tile([P, PAIR], F32)
         squares = consts.tile([P, CHUNK], BF16)
         y_mx = {}
         w_mx = {}
-        last_tile = (CH_TILES - 1, CHUNKS - 1)
+        last_pair = range(CH_TILES - PAIR, CH_TILES)
+
+        def chunk_stats(m, c, width=BN_STATS_DIM):
+            first = STATS_FIRST + c * BN_STATS_DIM
+            return stats[:, m, first : first + width]
 
         def aggregate_pair(pair):
             for m in range(pair * PAIR, (pair + 1) * PAIR):
-                used = CHUNKS * BN_STATS_DIM - (TRIPLE if m == last_tile[0] else 0)
-                nc.vector.bn_aggr(out=mean_var[:, :, m], in_=stats[:, m].rearrange("p c s -> p (c s)")[:, :used])
+                used = CHUNKS * BN_STATS_DIM - (TRIPLE if m in last_pair else 0)
+                nc.vector.bn_aggr(out=mean_var[:, :, m], in_=stats[:, m, STATS_FIRST : STATS_FIRST + used])
 
-        def scalar_stats(wy_last):
-            m, c = last_tile
-            tile_mean = stats[:, m, c, 1:2]
-            nc.scalar.activation(out=tile_mean, in_=last_sum[:], func=ACT.Copy, scale=1.0 / CHUNK)
+        def last_mean(m):
+            nc.gpsimd.tensor_scalar(
+                out=chunk_stats(m, CHUNKS - 1)[:, 1:2],
+                in0=last_sums[:, m % PAIR : m % PAIR + 1],
+                scalar1=1.0 / CHUNK,
+                scalar2=0.0,
+                op0=ALU.mult,
+                op1=ALU.add,
+            )
+
+        def last_squares(m, wy_last):
+            triple = chunk_stats(m, CHUNKS - 1, TRIPLE)
             nc.scalar.activation(
-                out=squares[:], in_=wy_last, func=ACT.Square, bias=tile_mean, scale=-1.0, accum_out=stats[:, m, c, 2:3]
+                out=squares[:], in_=wy_last, func=ACT.Square, bias=triple[:, 1:2], scale=-1.0, accum_out=triple[:, 2:3]
             )
 
         def multiply(m, c, wy):
@@ -175,20 +189,21 @@ def tile_nonlocalblocknd_pc_kernel(tc, y, w_w, w_b, bn_gamma, out_0, out_1, out_
                 start=True,
                 stop=True,
             )
-            if (m, c) == last_tile:
+            if m in last_pair and c == CHUNKS - 1:
                 nc.scalar.activation(
                     out=wy[:, t, :],
                     in_=acc[:],
                     func=ACT.Identity,
                     bias=bias_bf16[:, m : m + 1],
                     scale=1.0,
-                    accum_out=last_sum[:],
+                    accum_out=last_sums[:, t : t + 1],
                 )
+                last_mean(m)
             else:
                 nc.scalar.activation(
                     out=wy[:, t, :], in_=acc[:], func=ACT.Identity, bias=bias_bf16[:, m : m + 1], scale=1.0
                 )
-                nc.vector.bn_stats(out=stats[:, m, c, :], in_=wy[:, t, :])
+                nc.vector.bn_stats(out=chunk_stats(m, c), in_=wy[:, t, :])
 
         def keep_tensor_engine_busy(matmuls):
             acc = psum_acc.tile([P, CHUNK], F32)
@@ -215,7 +230,7 @@ def tile_nonlocalblocknd_pc_kernel(tc, y, w_w, w_b, bn_gamma, out_0, out_1, out_
                 if t == 0:
                     wy = wy_pool.tile([P, PAIR, CHUNK], F32)
                 multiply(m, c, wy)
-                if (pair, c) == (PAIRS - 1, CHUNKS - 1):
+                if (pair, c) in ((0, 0), (PAIRS - 1, CHUNKS - 1)):
                     nc.sync.dma_start(out=wy_rows[:, m, positions], in_=wy[:, t, :])
                 elif t == PAIR - 1:
                     nc.sync.dma_start(out=wy_rows[:, m - t : m + 1, positions], in_=wy[:])
@@ -227,7 +242,8 @@ def tile_nonlocalblocknd_pc_kernel(tc, y, w_w, w_b, bn_gamma, out_0, out_1, out_
                         y_grouped_next = regroup_y_chunk_on_gpsimd(c + 2)
                 if c == CHUNKS - 1 and t == PAIR - 1 and pair >= 1:
                     aggregate_pair(pair - 1)
-        scalar_stats(wy[:, PAIR - 1, :])
+        for m in last_pair:
+            last_squares(m, wy[:, m % PAIR, :])
         aggregate_pair(PAIRS - 1)
 
         inv_std = consts.tile([P, CH_TILES], F32)

@@ -28,7 +28,8 @@ BN_STATS_DIM = 6
 TRIPLE = 3
 STATS_FIRST = 6
 STATS_ROW = 32
-PREPARE_NEXT_AFTER_TILE = 3
+LAST_W_PAIR_AFTER_TILE = 2
+QUANTISE_NEXT_AFTER_TILE = (3, 2, 2)
 BN_EPS = 1e-5
 
 FLOPS = 2 * CHANNELS * D_IN * POSITIONS
@@ -189,7 +190,11 @@ def tile_nonlocalblocknd_pc_kernel(tc, y, w_w, w_b, bn_gamma, out_0, out_1, out_
                 start=True,
                 stop=True,
             )
-            if m in last_pair and c == CHUNKS - 1:
+            if (m, c) == (0, 0):
+                nc.vector.tensor_scalar(
+                    out=wy[:, t, :], in0=acc[:], scalar1=bias_bf16[:, m : m + 1], scalar2=None, op0=ALU.add
+                )
+            elif m in last_pair and c == CHUNKS - 1:
                 nc.scalar.activation(
                     out=wy[:, t, :],
                     in_=acc[:],
@@ -204,6 +209,8 @@ def tile_nonlocalblocknd_pc_kernel(tc, y, w_w, w_b, bn_gamma, out_0, out_1, out_
                     out=wy[:, t, :], in_=acc[:], func=ACT.Identity, bias=bias_bf16[:, m : m + 1], scale=1.0
                 )
                 nc.vector.bn_stats(out=chunk_stats(m, c), in_=wy[:, t, :])
+                if (m, c) == (1, 0):
+                    nc.vector.bn_stats(out=chunk_stats(0, c), in_=wy[:, 0, :])
 
         def keep_tensor_engine_busy(matmuls):
             acc = psum_acc.tile([P, CHUNK], F32)
@@ -234,9 +241,9 @@ def tile_nonlocalblocknd_pc_kernel(tc, y, w_w, w_b, bn_gamma, out_0, out_1, out_
                     nc.sync.dma_start(out=wy_rows[:, m, positions], in_=wy[:, t, :])
                 elif t == PAIR - 1:
                     nc.sync.dma_start(out=wy_rows[:, m - t : m + 1, positions], in_=wy[:])
-                if m == PREPARE_NEXT_AFTER_TILE and c == 0:
+                if m == LAST_W_PAIR_AFTER_TILE and c == 0:
                     w_mx[PAIRS - 1] = quantise_w_pair(transpose_w_pair(PAIRS - 1))
-                if m == PREPARE_NEXT_AFTER_TILE and c + 1 < CHUNKS:
+                if c + 1 < CHUNKS and m == QUANTISE_NEXT_AFTER_TILE[c]:
                     y_mx[c + 1] = quantise_y_chunk(y_grouped_next)
                     if c + 2 < CHUNKS:
                         y_grouped_next = regroup_y_chunk_on_gpsimd(c + 2)

@@ -29,7 +29,7 @@ TRIPLE = 3
 STATS_FIRST = 6
 STATS_ROW = 32
 LAST_W_PAIR_AFTER_TILE = 2
-QUANTISE_NEXT_AFTER_TILE = (3, 2, 2)
+QUANTISE_NEXT_AFTER_TILE = (4, 3, 2)
 BN_EPS = 1e-5
 
 FLOPS = 2 * CHANNELS * D_IN * POSITIONS

from contextlib import ExitStack

import concourse.mybir as mybir
from concourse.masks import make_identity

FP8X4 = mybir.dt.float8_e4m3fn_x4
BF16 = mybir.dt.bfloat16
F32 = mybir.dt.float32
U32 = mybir.dt.uint32
U8 = mybir.dt.uint8
ACT = mybir.ActivationFunctionType
ALU = mybir.AluOpType

P = 128
PACK = 4
D_IN = P * PACK
CHANNELS = 1024
POSITIONS = 2048
CH_TILES = CHANNELS // P
CHUNK = 512
CHUNKS = POSITIONS // CHUNK
PAIR = 2
PAIRS = CH_TILES // PAIR
RUN = 4
VECTOR_COLS = 384
GPSIMD_PIECE = 128
BN_STATS_DIM = 6
TRIPLE = 3
STATS_FIRST = 6
STATS_ROW = 32
LAST_W_PAIR_AFTER_TILE = 2
QUANTISE_NEXT_AFTER_TILE = (4, 3, 2)
BN_EPS = 1e-5

FLOPS = 2 * CHANNELS * D_IN * POSITIONS


def tile_nonlocalblocknd_pc_kernel(tc, y, w_w, w_b, bn_gamma, out_0, out_1, out_2):
    nc = tc.nc

    y_rows = y[0].rearrange("(p j) t h w -> p j (t h w)", j=PACK)
    w_rows = w_w.rearrange("(p m) d -> p (m d)", m=CH_TILES)
    wy_rows = out_0[0].rearrange("(p m) t h w -> p m (t h w)", m=CH_TILES)

    with ExitStack() as ctx:
        consts = ctx.enter_context(tc.tile_pool(name="consts", bufs=1))
        y_pool = ctx.enter_context(tc.tile_pool(name="y_pool", bufs=CHUNKS))
        w_pool = ctx.enter_context(tc.tile_pool(name="w_pool", bufs=PAIRS))
        handoff = ctx.enter_context(tc.tile_pool(name="handoff", bufs=1))
        wy_pool = ctx.enter_context(tc.tile_pool(name="wy_pool", bufs=PAIRS * CHUNKS))
        psum_w = ctx.enter_context(tc.psum_pool(name="psum_w", bufs=2))
        psum_acc = ctx.enter_context(tc.psum_pool(name="psum_acc", bufs=6))
        ctx.enter_context(tc.manual_schedule())

        def load_y_chunk(c):
            y_raw = y_pool.tile([P, PACK, CHUNK], BF16)
            nc.sync.dma_start(out=y_raw[:], in_=y_rows[:, :, c * CHUNK : (c + 1) * CHUNK])
            return y_raw

        def load_w_pair(pair):
            width = PAIR * D_IN
            w_raw = w_pool.tile([P, width], BF16)
            nc.sync.dma_start(out=w_raw[:], in_=w_rows[:, pair * width : (pair + 1) * width])
            return w_raw

        y_raws = {}
        w_raws = {}
        w_raws[0] = load_w_pair(0)
        y_raws[0] = load_y_chunk(0)
        w_raws[1] = load_w_pair(1)
        w_raws[2] = load_w_pair(2)
        y_raws[1] = load_y_chunk(1)
        w_raws[3] = load_w_pair(3)
        y_late = consts.tile([P, PACK, 2 * CHUNK], BF16)
        nc.sync.dma_start(out=y_late[:], in_=y_rows[:, :, 2 * CHUNK :])

        zeros = consts.tile([P, CHUNK], BF16)
        nc.gpsimd.memset(zeros[:], 0.0)
        eps = consts.tile([P, 1], F32)
        nc.vector.memset(eps[:], BN_EPS)
        stats = consts.tile([P, CH_TILES, STATS_ROW], F32)
        nc.vector.memset(stats[:], float(CHUNK))
        table_warmer = consts.tile([P, 1], F32)
        nc.scalar.activation(out=table_warmer[:], in_=eps[:], func=ACT.Abs_reciprocal_sqrt)
        bias_bf16 = consts.tile([P, CH_TILES], BF16)
        nc.scalar.dma_start(out=bias_bf16[:], in_=w_b.rearrange("(p m) -> p m", m=CH_TILES))
        gamma_bf16 = consts.tile([P, CH_TILES], BF16)
        nc.scalar.dma_start(out=gamma_bf16[:], in_=bn_gamma.rearrange("(p m) -> p m", m=CH_TILES))
        identity = consts.tile([P, P], F32)
        make_identity(nc, identity[:])

        def regroup_y_chunk(c):
            y_grouped = y_pool.tile([P, CHUNK, PACK], BF16, align_bytes=64)
            src = y_raws[c][:].rearrange("p j (c i) -> p c j i", i=RUN)
            dst = y_grouped[:].rearrange("p (c i) j -> p c j i", i=RUN)
            split = VECTOR_COLS // RUN
            nc.vector.tensor_copy(out=dst[:, :split], in_=src[:, :split])
            nc.scalar.copy(out=dst[:, split:], in_=src[:, split:])
            return y_grouped

        def regroup_y_chunk_on_gpsimd(c):
            y_grouped = handoff.tile([P, CHUNK, PACK], BF16, align_bytes=64)
            rows = y_raws[c][:] if c < 2 else y_late[:, :, (c - 2) * CHUNK : (c - 1) * CHUNK]
            for first in range(0, CHUNK, GPSIMD_PIECE):
                cols = slice(first, first + GPSIMD_PIECE)
                nc.gpsimd.tensor_scalar(
                    out=y_grouped[:, cols, :],
                    in0=rows[:, :, cols].rearrange("p j n -> p n j"),
                    scalar1=1.0,
                    scalar2=0.0,
                    op0=ALU.mult,
                    op1=ALU.add,
                )
            return y_grouped

        def quantise_y_chunk(y_grouped):
            y_codes = y_pool.tile([P, CHUNK], U32, align_bytes=64)
            y_scales = y_pool.tile([P, CHUNK], U8, align_bytes=64)
            nc.vector.quantize_mx(
                out=y_codes[:].bitcast(FP8X4),
                scales=y_scales[:],
                in_=y_grouped[:].rearrange("p n j -> p (n j)"),
            )
            return y_codes, y_scales

        def transpose_w_pair(pair):
            words = w_raws[pair][:].bitcast(F32).rearrange("c (t p u) -> c t u p", p=P, u=2)
            w_t = psum_w.tile([P, PAIR, 2, P], F32)
            for t in range(PAIR):
                for u in range(2):
                    nc.tensor.transpose(w_t[:, t, u, :], words[:, t, u, :], identity[:])
            w_grouped = w_pool.tile([P, PAIR * P * PACK], BF16, align_bytes=64)
            nc.scalar.copy(
                out=w_grouped[:].bitcast(F32).rearrange("p (t c u) -> p t c u", t=PAIR, u=2),
                in_=w_t[:].rearrange("p t u c -> p t c u"),
            )
            return w_grouped

        def quantise_w_pair(w_grouped):
            w_codes = w_pool.tile([P, PAIR * P], U32, align_bytes=64)
            w_scales = w_pool.tile([P, PAIR * P], U8, align_bytes=64)
            nc.vector.quantize_mx(out=w_codes[:].bitcast(FP8X4), scales=w_scales[:], in_=w_grouped[:])
            return w_codes, w_scales


        mean_var = consts.tile([P, 2, CH_TILES], F32)
        last_sums = consts.tile([P, PAIR], F32)
        squares = consts.tile([P, CHUNK], BF16)
        y_mx = {}
        w_mx = {}
        last_pair = range(CH_TILES - PAIR, CH_TILES)

        def chunk_stats(m, c, width=BN_STATS_DIM):
            first = STATS_FIRST + c * BN_STATS_DIM
            return stats[:, m, first : first + width]

        def aggregate_pair(pair):
            for m in range(pair * PAIR, (pair + 1) * PAIR):
                used = CHUNKS * BN_STATS_DIM - (TRIPLE if m in last_pair else 0)
                nc.vector.bn_aggr(out=mean_var[:, :, m], in_=stats[:, m, STATS_FIRST : STATS_FIRST + used])

        def last_mean(m):
            nc.gpsimd.tensor_scalar(
                out=chunk_stats(m, CHUNKS - 1)[:, 1:2],
                in0=last_sums[:, m % PAIR : m % PAIR + 1],
                scalar1=1.0 / CHUNK,
                scalar2=0.0,
                op0=ALU.mult,
                op1=ALU.add,
            )

        def last_squares(m, wy_last):
            triple = chunk_stats(m, CHUNKS - 1, TRIPLE)
            nc.scalar.activation(
                out=squares[:], in_=wy_last, func=ACT.Square, bias=triple[:, 1:2], scale=-1.0, accum_out=triple[:, 2:3]
            )

        def multiply(m, c, wy):
            pair, t = divmod(m, PAIR)
            w_codes, w_scales = w_mx[pair]
            y_codes, y_scales = y_mx[c]
            w_cols = slice(t * P, (t + 1) * P)
            acc = psum_acc.tile([P, CHUNK], F32)
            nc.tensor.matmul_mx(
                out=acc[:],
                lhsT=w_codes[:, w_cols].bitcast(FP8X4),
                lhsT_scale=w_scales[:, w_cols],
                rhs=y_codes[:].bitcast(FP8X4),
                rhs_scale=y_scales[:],
                start=True,
                stop=True,
            )
            if (m, c) == (0, 0):
                nc.vector.tensor_scalar(
                    out=wy[:, t, :], in0=acc[:], scalar1=bias_bf16[:, m : m + 1], scalar2=None, op0=ALU.add
                )
            elif m in last_pair and c == CHUNKS - 1:
                nc.scalar.activation(
                    out=wy[:, t, :],
                    in_=acc[:],
                    func=ACT.Identity,
                    bias=bias_bf16[:, m : m + 1],
                    scale=1.0,
                    accum_out=last_sums[:, t : t + 1],
                )
                last_mean(m)
            else:
                nc.scalar.activation(
                    out=wy[:, t, :], in_=acc[:], func=ACT.Identity, bias=bias_bf16[:, m : m + 1], scale=1.0
                )
                nc.vector.bn_stats(out=chunk_stats(m, c), in_=wy[:, t, :])
                if (m, c) == (1, 0):
                    nc.vector.bn_stats(out=chunk_stats(0, c), in_=wy[:, 0, :])

        def keep_tensor_engine_busy(matmuls):
            acc = psum_acc.tile([P, CHUNK], F32)
            for i in range(matmuls):
                nc.tensor.matmul(acc[:], lhsT=zeros[:, :P], rhs=zeros[:], start=True, stop=True)

        keep_tensor_engine_busy(4)
        w_grouped_0 = transpose_w_pair(0)
        keep_tensor_engine_busy(3)
        y_grouped_0 = regroup_y_chunk(0)
        w_mx[0] = quantise_w_pair(w_grouped_0)
        w_grouped_1 = transpose_w_pair(1)
        y_mx[0] = quantise_y_chunk(y_grouped_0)
        w_grouped_2 = transpose_w_pair(2)
        keep_tensor_engine_busy(1)
        w_mx[1] = quantise_w_pair(w_grouped_1)
        w_mx[2] = quantise_w_pair(w_grouped_2)
        y_grouped_next = regroup_y_chunk_on_gpsimd(1)

        for c in range(CHUNKS):
            positions = slice(c * CHUNK, (c + 1) * CHUNK)
            for m in range(CH_TILES):
                pair, t = divmod(m, PAIR)
                if t == 0:
                    wy = wy_pool.tile([P, PAIR, CHUNK], F32)
                multiply(m, c, wy)
                if (pair, c) in ((0, 0), (PAIRS - 1, CHUNKS - 1)):
                    nc.sync.dma_start(out=wy_rows[:, m, positions], in_=wy[:, t, :])
                elif t == PAIR - 1:
                    nc.sync.dma_start(out=wy_rows[:, m - t : m + 1, positions], in_=wy[:])
                if m == LAST_W_PAIR_AFTER_TILE and c == 0:
                    w_mx[PAIRS - 1] = quantise_w_pair(transpose_w_pair(PAIRS - 1))
                if c + 1 < CHUNKS and m == QUANTISE_NEXT_AFTER_TILE[c]:
                    y_mx[c + 1] = quantise_y_chunk(y_grouped_next)
                    if c + 2 < CHUNKS:
                        y_grouped_next = regroup_y_chunk_on_gpsimd(c + 2)
                if c == CHUNKS - 1 and t == PAIR - 1 and pair >= 1:
                    aggregate_pair(pair - 1)
        for m in last_pair:
            last_squares(m, wy[:, m % PAIR, :])
        aggregate_pair(PAIRS - 1)

        inv_std = consts.tile([P, CH_TILES], F32)
        nc.scalar.activation(
            out=inv_std[:], in_=mean_var[:, 1, :], func=ACT.Abs_reciprocal_sqrt, bias=eps[:], scale=1.0
        )
        nc.scalar.dma_start(out=out_1.rearrange("(p m) -> p m", m=CH_TILES), in_=mean_var[:, 0, :])
        gain = consts.tile([P, CH_TILES], F32)
        nc.vector.tensor_mul(out=gain[:], in0=inv_std[:], in1=gamma_bf16[:])
        nc.scalar.dma_start(out=out_2.rearrange("(p m) -> p m", m=CH_TILES), in_=gain[:])
